import numpy as np
import ml_dtypes


def mxq(x, axis, fmt="e4m3"):
    dtype, down = {"e4m3": (ml_dtypes.float8_e4m3fn, 7), "e5m2": (ml_dtypes.float8_e5m2, 14)}[fmt]
    v = np.moveaxis(np.asarray(x, np.float32).astype(ml_dtypes.bfloat16).astype(np.float64), axis, -1)
    blocks = v.reshape(v.shape[:-1] + (-1, 32))
    amax = np.abs(blocks).max(-1, keepdims=True)
    byte = np.maximum(np.where(amax > 0, np.frexp(amax)[1] - 1 + 127, 0) - down, 1)
    scale = np.exp2(byte - 127.0)
    codes = (blocks / scale).astype(np.float32).astype(dtype).astype(np.float64)
    return np.moveaxis((codes * scale).reshape(v.shape), -1, axis)


WIDE = False


def mx_kscale(k):
    if not WIDE:
        return np.ones(k)
    levels = np.array([10, -10, 5, -5, 0])
    a = np.random.permutation(np.resize(levels, k // 512 * 4)).reshape(k // 512, 4)
    idx = np.arange(k)
    return np.exp2(a[idx // 512, idx % 128 // 32])


BF16 = ml_dtypes.bfloat16


def bf(x):
    return np.asarray(x, np.float32).astype(BF16)


def f64(x):
    return np.asarray(x).astype(np.float64)


E2M1 = np.array([0.0, 0.5, 1.0, 1.5, 2.0, 3.0, 4.0, 6.0, -0.0, -0.5, -1.0, -1.5, -2.0, -3.0, -4.0, -6.0])


def pack_weight(w, fmt):
    k, n = w.shape
    w = f64(bf(w)).reshape(k // 32, 32, n)
    amax = np.abs(w).max(1)
    if fmt == "e4m3":
        byte = np.frexp(amax)[1] - 1 + 127 - 7
    else:
        mant, ex = np.frexp(amax / 6.0)
        byte = np.where(mant > 0.5, ex, ex - 1) + 127
    byte = np.clip(np.where(amax > 0, byte, 1), 1, 254)
    scaled = (w * np.exp2(127.0 - byte)[:, None, :]).reshape(k, n).astype(np.float32)
    by_word = np.ascontiguousarray(scaled.reshape(k // 512, 128, 4, n).transpose(0, 1, 3, 2))
    if fmt == "e4m3":
        words = by_word.astype(ml_dtypes.float8_e4m3fn).view(np.uint8)
    else:
        c = by_word.astype(ml_dtypes.float4_e2m1fn).view(np.uint8) & 0xF
        words = c[..., 0::2] | (c[..., 1::2] << 4)
    return np.ascontiguousarray(words), np.ascontiguousarray(byte.astype(np.uint8).reshape(k // 512, 16, n))


def unpack_weight(words, scales, fmt):
    g, p, n, _ = words.shape
    if fmt == "e4m3":
        vals = np.ascontiguousarray(words).view(ml_dtypes.float8_e4m3fn).astype(np.float64)
    else:
        nib = np.empty((g, p, n, 4), np.uint8)
        nib[..., 0::2] = words & 0xF
        nib[..., 1::2] = words >> 4
        vals = E2M1[nib]
    vals = vals * np.repeat(np.exp2(scales.astype(np.float64) - 127.0), 8, axis=1)[..., None]
    return vals.transpose(0, 1, 3, 2).reshape(g * 512, n)


N, D, DO, R0, R1, R2, R3, R4 = 2560, 512, 512, 1, 2, 4, 10, 25
SCALES = (R0, R1, R2, R3)
NS = len(SCALES)
FMT = "e4m3"


def setup_inputs():
    s = mx_kscale(D)
    x = bf(np.random.standard_normal((N, D)) * s)
    stack = np.random.standard_normal((NS, DO, D)) / np.sqrt(D) / s
    cat = np.ascontiguousarray(stack.swapaxes(1, 2)).reshape(-1, DO)
    words, scales = pack_weight(cat, FMT)
    bs = bf(np.random.standard_normal((NS, DO)) * 0.5)
    return {"inputs_c_e": x,
            "Ws_words": words,
            "Ws_scales": scales,
            "bs": bs}


def reference(inputs_c_e, Ws_words, Ws_scales, bs):
    x, b = f64(inputs_c_e), f64(bs)
    Wt = unpack_weight(Ws_words, Ws_scales, FMT).reshape(NS, D, DO)
    outs = []
    for i, r in enumerate(SCALES):
        groups = N // r
        sums = x.reshape(groups, r, D).sum(axis=1)
        h = np.maximum((mxq(sums, 1, "e4m3") @ Wt[i]) + b[i], 0.0) / r
        outs.append(np.repeat(h, r, axis=0))
    return np.concatenate(outs, axis=0)

@@ -1,0 +1,196 @@
+from contextlib import ExitStack
+
+from concourse import mybir
+from concourse.masks import make_identity
+
+F32 = mybir.dt.float32
+BF16 = mybir.dt.bfloat16
+I32 = mybir.dt.int32
+U32 = mybir.dt.uint32
+U8 = mybir.dt.uint8
+FP8X4 = mybir.dt.float8_e4m3fn_x4
+ADD = mybir.AluOpType.add
+RELU = mybir.ActivationFunctionType.Relu
+
+P = 128
+PACK = 4
+N_ROWS = 2560
+D = 512
+DO = 512
+GROUP_LENGTHS = (1, 2, 4, 10)
+ROWS_PER_PARTITION = N_ROWS // P
+CHUNK = 4
+CHUNKS = ROWS_PER_PARTITION // CHUNK
+UNIT = 2
+
+FLOPS = 2 * sum(N_ROWS // r for r in GROUP_LENGTHS) * D * DO
+
+
+def tile_contractexpand_pa_e_kernel(tc, inputs_c_e, Ws_words, Ws_scales, bs, out):
+    nc = tc.nc
+    scales_n = len(GROUP_LENGTHS)
+
+    x_rows = inputs_c_e.rearrange("(p j) d -> p j d", j=ROWS_PER_PARTITION)
+    out_rows = out.rearrange("(i p j) n -> i p j n", i=scales_n, j=ROWS_PER_PARTITION)
+
+    with ExitStack() as ctx:
+        keep = ctx.enter_context(tc.tile_pool(name="keep", bufs=1))
+        stage = ctx.enter_context(tc.tile_pool(name="stage", bufs=4))
+        results = ctx.enter_context(tc.tile_pool(name="results", bufs=22))
+        psum_t = ctx.enter_context(tc.psum_pool(name="psum_t", bufs=4))
+        psum_mm = ctx.enter_context(tc.psum_pool(name="psum_mm", bufs=4))
+
+        w_planes = keep.tile([P, DO], U8, name="w_planes", align_bytes=64)
+        nc.vector.memset(w_planes[:].bitcast(I32), 0)
+        bias_row = keep.tile([P, scales_n * DO], BF16, name="bias_row")
+        nc.vector.memset(bias_row[:], 0.0)
+        ones = keep.tile([P, P], BF16, name="ones")
+        nc.vector.memset(ones[:], 1.0)
+        ident = keep.tile([P, P], F32, name="ident")
+        make_identity(nc, ident[:])
+
+        x_chunks = [keep.tile([P, CHUNK, D], BF16, name="x%d" % c) for c in range(CHUNKS)]
+        w_words = keep.tile([P, scales_n, DO], U32, name="w_words", align_bytes=64)
+
+        def load_x(c):
+            nc.sync.dma_start(out=x_chunks[c][:], in_=x_rows[:, c * CHUNK : (c + 1) * CHUNK, :])
+
+        def load_w(g):
+            nc.sync.dma_start(
+                out=w_words[:, g, :].bitcast(I32),
+                in_=Ws_words[g].rearrange("p n t -> p (n t)").bitcast(I32),
+            )
+
+        load_x(0)
+        for quad in range(4):
+            nc.sync.dma_start(
+                out=w_planes[32 * quad : 32 * quad + 16, :].bitcast(I32),
+                in_=Ws_scales[:, 4 * quad : 4 * quad + 4, :].bitcast(I32),
+            )
+        nc.sync.dma_start(out=bias_row[0:1, :], in_=bs.rearrange("(o i) n -> o (i n)", o=1))
+        load_w(0)
+        load_x(1)
+        load_w(1)
+        load_w(2)
+        load_x(2)
+        load_w(3)
+        load_x(3)
+        load_x(4)
+
+        bias_all = keep.tile([P, scales_n, DO], F32, name="bias_all")
+        for i in range(scales_n):
+            spread = psum_mm.tile([P, DO], F32, tag="acc")
+            nc.tensor.matmul(
+                out=spread[:], lhsT=ones[:], rhs=bias_row[:, i * DO : (i + 1) * DO], start=True, stop=True
+            )
+            nc.scalar.copy(out=bias_all[:, i, :], in_=spread[:])
+
+        pair_sums = [keep.tile([P, CHUNK // 2, D], F32, name="pair%d" % c) for c in range(CHUNKS)]
+        four_sums = [keep.tile([P, D], F32, name="four%d" % c) for c in range(CHUNKS)]
+        ten_sums = [keep.tile([P, D], F32, name="ten%d" % h) for h in range(2)]
+
+        def sum_chunk(c):
+            halves = x_chunks[c][:].rearrange("p (m e) (q t) -> p e m t q", e=2, t=PACK)
+            nc.vector.tensor_tensor(
+                out=pair_sums[c][:].rearrange("p m (t q) -> p m t q", t=PACK),
+                in0=halves[:, 0],
+                in1=halves[:, 1],
+                op=ADD,
+            )
+            nc.vector.tensor_tensor(
+                out=four_sums[c][:], in0=pair_sums[c][:, 0, :], in1=pair_sums[c][:, 1, :], op=ADD
+            )
+
+        def sum_ten(h):
+            nc.vector.tensor_tensor(
+                out=ten_sums[h][:], in0=four_sums[3 * h][:], in1=four_sums[3 * h + 1][:], op=ADD
+            )
+            nc.vector.tensor_tensor(
+                out=ten_sums[h][:], in0=ten_sums[h][:], in1=pair_sums[2][:, h, :], op=ADD
+            )
+
+        def summed(i, m):
+            if i == 1:
+                return pair_sums[m // 2][:, m % 2, :]
+            if i == 2:
+                return four_sums[m][:]
+            return ten_sums[m][:]
+
+        def front(i, first, count):
+            grouped = stage.tile([P, UNIT * D], BF16, tag="grouped", align_bytes=64)
+            if i == 0:
+                flipped = psum_t.tile([P, 2 * count, P], F32, tag="flipped")
+                for a in range(count):
+                    row = first + a
+                    words = x_chunks[row // CHUNK][:, row % CHUNK, :].bitcast(F32)
+                    for u in range(2):
+                        nc.tensor.transpose(flipped[:, 2 * a + u, :], words[:, u : D // 2 : 2], ident[:])
+                nc.scalar.copy(
+                    out=grouped[:].bitcast(F32).rearrange("q (a r u) -> q a r u", a=count, u=2),
+                    in_=flipped[:].rearrange("q (a u) r -> q a r u", u=2),
+                )
+            else:
+                for a in range(count):
+                    flipped = psum_t.tile([P, PACK, P], F32, tag="flipped")
+                    source = summed(i, first + a)
+                    for t in range(PACK):
+                        nc.tensor.transpose(flipped[:, t, :], source[:, t * P : (t + 1) * P], ident[:])
+                    nc.scalar.copy(
+                        out=grouped[:, a * D : (a + 1) * D].rearrange("q (r t) -> q r t", t=PACK),
+                        in_=flipped[:].rearrange("q t r -> q r t"),
+                    )
+            codes = stage.tile([P, UNIT * P], U32, tag="codes", align_bytes=64)
+            planes = stage.tile([P, UNIT * P], U8, tag="planes", align_bytes=64)
+            nc.vector.quantize_mx(
+                out=codes[:, : count * P].bitcast(FP8X4),
+                scales=planes[:, : count * P],
+                in_=grouped[:, : count * D],
+            )
+            return codes, planes
+
+        def back(i, first, count, codes, planes):
+            r = GROUP_LENGTHS[i]
+            res = results.tile([P, UNIT, DO], F32, tag="res")
+            for a in range(count):
+                acc = psum_mm.tile([P, DO], F32, tag="acc")
+                nc.tensor.matmul_mx(
+                    out=acc[:],
+                    lhsT=codes[:, a * P : (a + 1) * P].bitcast(FP8X4),
+                    lhsT_scale=planes[:, a * P : (a + 1) * P],
+                    rhs=w_words[:, i, :].bitcast(FP8X4),
+                    rhs_scale=w_planes[4 * i : P, :],
+                    start=True,
+                    stop=True,
+                )
+                nc.vector.tensor_tensor(out=res[:, a, :], in0=acc[:], in1=bias_all[:, i, :], op=ADD)
+            nc.scalar.activation(out=res[:, :count, :], in_=res[:, :count, :], func=RELU, scale=1.0 / r)
+            if r == 1:
+                nc.sync.dma_start(out=out_rows[i][:, first : first + count, :], in_=res[:, :count, :])
+            else:
+                for a in range(count):
+                    m = first + a
+                    nc.sync.dma_start(
+                        out=out_rows[i][:, m * r : (m + 1) * r, :],
+                        in_=res[:, a : a + 1, :].to_broadcast([P, r, DO]),
+                    )
+
+        units = []
+        for c in range(CHUNKS):
+            for i, r in enumerate(GROUP_LENGTHS):
+                ready = [m for m in range(ROWS_PER_PARTITION // r) if (m * r + r - 1) // CHUNK == c]
+                for k in range(0, len(ready), UNIT):
+                    units.append((c, i, ready[k], len(ready[k : k + UNIT])))
+
+        summed_chunks = 0
+        waiting = None
+        for c, i, first, count in units:
+            if c == summed_chunks:
+                sum_chunk(c)
+                summed_chunks += 1
+            if i == 3:
+                sum_ten(first)
+            quantised = front(i, first, count)
+            if waiting is not None:
+                back(*waiting)
+            waiting = (i, first, count) + quantised
+        back(*waiting)

@@ -10,6 +10,8 @@ U32 = mybir.dt.uint32
 U8 = mybir.dt.uint8
 FP8X4 = mybir.dt.float8_e4m3fn_x4
 ADD = mybir.AluOpType.add
+MAX = mybir.AluOpType.max
+MULT = mybir.AluOpType.mult
 RELU = mybir.ActivationFunctionType.Relu
 
 P = 128
@@ -36,7 +38,7 @@ def tile_contractexpand_pa_e_kernel(tc, inputs_c_e, Ws_words, Ws_scales, bs, out
     with ExitStack() as ctx:
         keep = ctx.enter_context(tc.tile_pool(name="keep", bufs=1))
         stage = ctx.enter_context(tc.tile_pool(name="stage", bufs=4))
-        results = ctx.enter_context(tc.tile_pool(name="results", bufs=22))
+        results = ctx.enter_context(tc.tile_pool(name="results", bufs=23))
         psum_t = ctx.enter_context(tc.psum_pool(name="psum_t", bufs=4))
         psum_mm = ctx.enter_context(tc.psum_pool(name="psum_mm", bufs=4))
 
@@ -61,13 +63,13 @@ def tile_contractexpand_pa_e_kernel(tc, inputs_c_e, Ws_words, Ws_scales, bs, out
                 in_=Ws_words[g].rearrange("p n t -> p (n t)").bitcast(I32),
             )
 
+        nc.sync.dma_start(out=bias_row[0:1, :], in_=bs.rearrange("(o i) n -> o (i n)", o=1))
         load_x(0)
         for quad in range(4):
             nc.sync.dma_start(
                 out=w_planes[32 * quad : 32 * quad + 16, :].bitcast(I32),
                 in_=Ws_scales[:, 4 * quad : 4 * quad + 4, :].bitcast(I32),
             )
-        nc.sync.dma_start(out=bias_row[0:1, :], in_=bs.rearrange("(o i) n -> o (i n)", o=1))
         load_w(0)
         load_x(1)
         load_w(1)
@@ -83,7 +85,7 @@ def tile_contractexpand_pa_e_kernel(tc, inputs_c_e, Ws_words, Ws_scales, bs, out
             nc.tensor.matmul(
                 out=spread[:], lhsT=ones[:], rhs=bias_row[:, i * DO : (i + 1) * DO], start=True, stop=True
             )
-            nc.scalar.copy(out=bias_all[:, i, :], in_=spread[:])
+            nc.vector.tensor_copy(out=bias_all[:, i, :], in_=spread[:])
 
         pair_sums = [keep.tile([P, CHUNK // 2, D], F32, name="pair%d" % c) for c in range(CHUNKS)]
         four_sums = [keep.tile([P, D], F32, name="four%d" % c) for c in range(CHUNKS)]
@@ -91,21 +93,21 @@ def tile_contractexpand_pa_e_kernel(tc, inputs_c_e, Ws_words, Ws_scales, bs, out
 
         def sum_chunk(c):
             halves = x_chunks[c][:].rearrange("p (m e) (q t) -> p e m t q", e=2, t=PACK)
-            nc.vector.tensor_tensor(
+            nc.gpsimd.tensor_tensor(
                 out=pair_sums[c][:].rearrange("p m (t q) -> p m t q", t=PACK),
                 in0=halves[:, 0],
                 in1=halves[:, 1],
                 op=ADD,
             )
-            nc.vector.tensor_tensor(
+            nc.gpsimd.tensor_tensor(
                 out=four_sums[c][:], in0=pair_sums[c][:, 0, :], in1=pair_sums[c][:, 1, :], op=ADD
             )
 
         def sum_ten(h):
-            nc.vector.tensor_tensor(
+            nc.gpsimd.tensor_tensor(
                 out=ten_sums[h][:], in0=four_sums[3 * h][:], in1=four_sums[3 * h + 1][:], op=ADD
             )
-            nc.vector.tensor_tensor(
+            nc.gpsimd.tensor_tensor(
                 out=ten_sums[h][:], in0=ten_sums[h][:], in1=pair_sums[2][:, h, :], op=ADD
             )
 
@@ -126,7 +128,7 @@ def tile_contractexpand_pa_e_kernel(tc, inputs_c_e, Ws_words, Ws_scales, bs, out
                     for u in range(2):
                         nc.tensor.transpose(flipped[:, 2 * a + u, :], words[:, u : D // 2 : 2], ident[:])
                 nc.scalar.copy(
-                    out=grouped[:].bitcast(F32).rearrange("q (a r u) -> q a r u", a=count, u=2),
+                    out=grouped[:, : count * D].bitcast(F32).rearrange("q (a r u) -> q a r u", a=count, u=2),
                     in_=flipped[:].rearrange("q (a u) r -> q a r u", u=2),
                 )
             else:
@@ -163,7 +165,12 @@ def tile_contractexpand_pa_e_kernel(tc, inputs_c_e, Ws_words, Ws_scales, bs, out
                     stop=True,
                 )
                 nc.vector.tensor_tensor(out=res[:, a, :], in0=acc[:], in1=bias_all[:, i, :], op=ADD)
-            nc.scalar.activation(out=res[:, :count, :], in_=res[:, :count, :], func=RELU, scale=1.0 / r)
+            if i == 1:
+                nc.vector.tensor_scalar(
+                    out=res[:, :count, :], in0=res[:, :count, :], scalar1=0.0, scalar2=1.0 / r, op0=MAX, op1=MULT
+                )
+            else:
+                nc.scalar.activation(out=res[:, :count, :], in_=res[:, :count, :], func=RELU, scale=1.0 / r)
             if r == 1:
                 nc.sync.dma_start(out=out_rows[i][:, first : first + count, :], in_=res[:, :count, :])
             else:
@@ -178,8 +185,10 @@ def tile_contractexpand_pa_e_kernel(tc, inputs_c_e, Ws_words, Ws_scales, bs, out
         for c in range(CHUNKS):
             for i, r in enumerate(GROUP_LENGTHS):
                 ready = [m for m in range(ROWS_PER_PARTITION // r) if (m * r + r - 1) // CHUNK == c]
-                for k in range(0, len(ready), UNIT):
-                    units.append((c, i, ready[k], len(ready[k : k + UNIT])))
+                while ready:
+                    count = min(len(ready), UNIT if units else 1)
+                    units.append((c, i, ready[0], count))
+                    ready = ready[count:]
 
         summed_chunks = 0
         waiting = None

@@ -23,7 +23,6 @@ GROUP_LENGTHS = (1, 2, 4, 10)
 ROWS_PER_PARTITION = N_ROWS // P
 CHUNK = 4
 CHUNKS = ROWS_PER_PARTITION // CHUNK
-UNIT = 2
 
 FLOPS = 2 * sum(N_ROWS // r for r in GROUP_LENGTHS) * D * DO
 
@@ -38,7 +37,6 @@ def tile_contractexpand_pa_e_kernel(tc, inputs_c_e, Ws_words, Ws_scales, bs, out
     with ExitStack() as ctx:
         keep = ctx.enter_context(tc.tile_pool(name="keep", bufs=1))
         stage = ctx.enter_context(tc.tile_pool(name="stage", bufs=4))
-        results = ctx.enter_context(tc.tile_pool(name="results", bufs=23))
         psum_t = ctx.enter_context(tc.psum_pool(name="psum_t", bufs=4))
         psum_mm = ctx.enter_context(tc.psum_pool(name="psum_mm", bufs=4))
 
@@ -52,40 +50,41 @@ def tile_contractexpand_pa_e_kernel(tc, inputs_c_e, Ws_words, Ws_scales, bs, out
         make_identity(nc, ident[:])
 
         x_chunks = [keep.tile([P, CHUNK, D], BF16, name="x%d" % c) for c in range(CHUNKS)]
-        w_words = keep.tile([P, scales_n, DO], U32, name="w_words", align_bytes=64)
+        w_words = [keep.tile([P, DO], U32, name="w%d" % g, align_bytes=64) for g in range(scales_n)]
 
         def load_x(c):
             nc.sync.dma_start(out=x_chunks[c][:], in_=x_rows[:, c * CHUNK : (c + 1) * CHUNK, :])
 
         def load_w(g):
             nc.sync.dma_start(
-                out=w_words[:, g, :].bitcast(I32),
+                out=w_words[g][:].bitcast(I32),
                 in_=Ws_words[g].rearrange("p n t -> p (n t)").bitcast(I32),
             )
 
-        nc.sync.dma_start(out=bias_row[0:1, :], in_=bs.rearrange("(o i) n -> o (i n)", o=1))
         load_x(0)
         for quad in range(4):
             nc.sync.dma_start(
                 out=w_planes[32 * quad : 32 * quad + 16, :].bitcast(I32),
                 in_=Ws_scales[:, 4 * quad : 4 * quad + 4, :].bitcast(I32),
             )
-        load_w(0)
-        load_x(1)
-        load_w(1)
+        nc.sync.dma_start(out=bias_row[0:1, :], in_=bs.rearrange("(o i) n -> o (i n)", o=1))
         load_w(2)
+        load_w(1)
+        load_x(1)
         load_x(2)
         load_w(3)
         load_x(3)
         load_x(4)
+        load_w(0)
 
-        bias_all = keep.tile([P, scales_n, DO], F32, name="bias_all")
-        for i in range(scales_n):
+        biases = [keep.tile([P, DO], F32, name="bias%d" % i) for i in range(scales_n)]
+
+        def spread_bias(i):
             spread = psum_mm.tile([P, DO], F32, tag="acc")
             nc.tensor.matmul(
                 out=spread[:], lhsT=ones[:], rhs=bias_row[:, i * DO : (i + 1) * DO], start=True, stop=True
             )
-            nc.vector.tensor_copy(out=bias_all[:, i, :], in_=spread[:])
+            nc.scalar.copy(out=biases[i][:], in_=spread[:])
 
         pair_sums = [keep.tile([P, CHUNK // 2, D], F32, name="pair%d" % c) for c in range(CHUNKS)]
         four_sums = [keep.tile([P, D], F32, name="four%d" % c) for c in range(CHUNKS)]
@@ -93,21 +92,21 @@ def tile_contractexpand_pa_e_kernel(tc, inputs_c_e, Ws_words, Ws_scales, bs, out
 
         def sum_chunk(c):
             halves = x_chunks[c][:].rearrange("p (m e) (q t) -> p e m t q", e=2, t=PACK)
-            nc.gpsimd.tensor_tensor(
+            nc.vector.tensor_tensor(
                 out=pair_sums[c][:].rearrange("p m (t q) -> p m t q", t=PACK),
                 in0=halves[:, 0],
                 in1=halves[:, 1],
                 op=ADD,
             )
-            nc.gpsimd.tensor_tensor(
+            nc.vector.tensor_tensor(
                 out=four_sums[c][:], in0=pair_sums[c][:, 0, :], in1=pair_sums[c][:, 1, :], op=ADD
             )
 
         def sum_ten(h):
-            nc.gpsimd.tensor_tensor(
+            nc.vector.tensor_tensor(
                 out=ten_sums[h][:], in0=four_sums[3 * h][:], in1=four_sums[3 * h + 1][:], op=ADD
             )
-            nc.gpsimd.tensor_tensor(
+            nc.vector.tensor_tensor(
                 out=ten_sums[h][:], in0=ten_sums[h][:], in1=pair_sums[2][:, h, :], op=ADD
             )
 
@@ -119,18 +118,21 @@ def tile_contractexpand_pa_e_kernel(tc, inputs_c_e, Ws_words, Ws_scales, bs, out
             return ten_sums[m][:]
 
         def front(i, first, count):
-            grouped = stage.tile([P, UNIT * D], BF16, tag="grouped", align_bytes=64)
+            grouped = stage.tile([P, CHUNK * D], BF16, tag="grouped", align_bytes=64)
             if i == 0:
-                flipped = psum_t.tile([P, 2 * count, P], F32, tag="flipped")
-                for a in range(count):
-                    row = first + a
-                    words = x_chunks[row // CHUNK][:, row % CHUNK, :].bitcast(F32)
-                    for u in range(2):
-                        nc.tensor.transpose(flipped[:, 2 * a + u, :], words[:, u : D // 2 : 2], ident[:])
-                nc.scalar.copy(
-                    out=grouped[:, : count * D].bitcast(F32).rearrange("q (a r u) -> q a r u", a=count, u=2),
-                    in_=flipped[:].rearrange("q (a u) r -> q a r u", u=2),
-                )
+                for b in range(count // 2):
+                    flipped = psum_t.tile([P, 4, P], F32, tag="flipped")
+                    for a in range(2):
+                        row = first + 2 * b + a
+                        words = x_chunks[row // CHUNK][:, row % CHUNK, :].bitcast(F32)
+                        for u in range(2):
+                            nc.tensor.transpose(flipped[:, 2 * a + u, :], words[:, u : D // 2 : 2], ident[:])
+                    nc.scalar.copy(
+                        out=grouped[:, 2 * b * D : 2 * (b + 1) * D]
+                        .bitcast(F32)
+                        .rearrange("q (a r u) -> q a r u", a=2, u=2),
+                        in_=flipped[:].rearrange("q (a u) r -> q a r u", u=2),
+                    )
             else:
                 for a in range(count):
                     flipped = psum_t.tile([P, PACK, P], F32, tag="flipped")
@@ -141,8 +143,8 @@ def tile_contractexpand_pa_e_kernel(tc, inputs_c_e, Ws_words, Ws_scales, bs, out
                         out=grouped[:, a * D : (a + 1) * D].rearrange("q (r t) -> q r t", t=PACK),
                         in_=flipped[:].rearrange("q t r -> q r t"),
                     )
-            codes = stage.tile([P, UNIT * P], U32, tag="codes", align_bytes=64)
-            planes = stage.tile([P, UNIT * P], U8, tag="planes", align_bytes=64)
+            codes = stage.tile([P, CHUNK * P], U32, tag="codes", align_bytes=64)
+            planes = stage.tile([P, CHUNK * P], U8, tag="planes", align_bytes=64)
             nc.vector.quantize_mx(
                 out=codes[:, : count * P].bitcast(FP8X4),
                 scales=planes[:, : count * P],
@@ -152,50 +154,60 @@ def tile_contractexpand_pa_e_kernel(tc, inputs_c_e, Ws_words, Ws_scales, bs, out
 
         def back(i, first, count, codes, planes):
             r = GROUP_LENGTHS[i]
-            res = results.tile([P, UNIT, DO], F32, tag="res")
+            if first == 0:
+                spread_bias(i)
+            biased = keep.tile([P, count, DO], F32, name="biased%d_%d" % (i, first))
             for a in range(count):
                 acc = psum_mm.tile([P, DO], F32, tag="acc")
                 nc.tensor.matmul_mx(
                     out=acc[:],
                     lhsT=codes[:, a * P : (a + 1) * P].bitcast(FP8X4),
                     lhsT_scale=planes[:, a * P : (a + 1) * P],
-                    rhs=w_words[:, i, :].bitcast(FP8X4),
+                    rhs=w_words[i][:].bitcast(FP8X4),
                     rhs_scale=w_planes[4 * i : P, :],
                     start=True,
                     stop=True,
                 )
-                nc.vector.tensor_tensor(out=res[:, a, :], in0=acc[:], in1=bias_all[:, i, :], op=ADD)
-            if i == 1:
+                nc.vector.tensor_tensor(out=biased[:, a, :], in0=acc[:], in1=biases[i][:], op=ADD)
+            if r == max(GROUP_LENGTHS):
+                repeated = keep.tile([P, r, DO], F32, name="repeated%d" % first)
                 nc.vector.tensor_scalar(
-                    out=res[:, :count, :], in0=res[:, :count, :], scalar1=0.0, scalar2=1.0 / r, op0=MAX, op1=MULT
+                    out=repeated[:],
+                    in0=biased[:].to_broadcast([P, r, DO]),
+                    scalar1=0.0,
+                    scalar2=1.0 / r,
+                    op0=MAX,
+                    op1=MULT,
                 )
-            else:
-                nc.scalar.activation(out=res[:, :count, :], in_=res[:, :count, :], func=RELU, scale=1.0 / r)
+                nc.sync.dma_start(out=out_rows[i][:, first * r : (first + 1) * r, :], in_=repeated[:])
+                return
+            nc.scalar.activation(out=biased[:], in_=biased[:], func=RELU, scale=1.0 / r)
             if r == 1:
-                nc.sync.dma_start(out=out_rows[i][:, first : first + count, :], in_=res[:, :count, :])
+                nc.sync.dma_start(out=out_rows[i][:, first : first + count, :], in_=biased[:])
             else:
                 for a in range(count):
                     m = first + a
                     nc.sync.dma_start(
                         out=out_rows[i][:, m * r : (m + 1) * r, :],
-                        in_=res[:, a : a + 1, :].to_broadcast([P, r, DO]),
+                        in_=biased[:, a : a + 1, :].to_broadcast([P, r, DO]),
                     )
+
+        def units_of(c, i):
+            r = GROUP_LENGTHS[i]
+            ready = [m for m in range(ROWS_PER_PARTITION // r) if (m * r + r - 1) // CHUNK == c]
+            return [(c, i, ready[0], len(ready))] if ready else []
 
         units = []
         for c in range(CHUNKS):
-            for i, r in enumerate(GROUP_LENGTHS):
-                ready = [m for m in range(ROWS_PER_PARTITION // r) if (m * r + r - 1) // CHUNK == c]
-                while ready:
-                    count = min(len(ready), UNIT if units else 1)
-                    units.append((c, i, ready[0], count))
-                    ready = ready[count:]
+            for i in (2, 1, 3):
+                units.extend(units_of(c, i))
+        for c in range(CHUNKS):
+            units.extend(units_of(c, 0))
 
-        summed_chunks = 0
         waiting = None
         for c, i, first, count in units:
-            if c == summed_chunks:
+            if i == 2:
                 sum_chunk(c)
-                summed_chunks += 1
             if i == 3:
                 sum_ten(first)
             quantised = front(i, first, count)

@@ -88,7 +88,6 @@ def tile_contractexpand_pa_e_kernel(tc, inputs_c_e, Ws_words, Ws_scales, bs, out
 
         pair_sums = [keep.tile([P, CHUNK // 2, D], F32, name="pair%d" % c) for c in range(CHUNKS)]
         four_sums = [keep.tile([P, D], F32, name="four%d" % c) for c in range(CHUNKS)]
-        ten_sums = [keep.tile([P, D], F32, name="ten%d" % h) for h in range(2)]
 
         def sum_chunk(c):
             halves = x_chunks[c][:].rearrange("p (m e) (q t) -> p e m t q", e=2, t=PACK)
@@ -102,20 +101,12 @@ def tile_contractexpand_pa_e_kernel(tc, inputs_c_e, Ws_words, Ws_scales, bs, out
                 out=four_sums[c][:], in0=pair_sums[c][:, 0, :], in1=pair_sums[c][:, 1, :], op=ADD
             )
 
-        def sum_ten(h):
-            nc.vector.tensor_tensor(
-                out=ten_sums[h][:], in0=four_sums[3 * h][:], in1=four_sums[3 * h + 1][:], op=ADD
-            )
-            nc.vector.tensor_tensor(
-                out=ten_sums[h][:], in0=ten_sums[h][:], in1=pair_sums[2][:, h, :], op=ADD
-            )
-
         def summed(i, m):
             if i == 1:
-                return pair_sums[m // 2][:, m % 2, :]
+                return [pair_sums[m // 2][:, m % 2, :]]
             if i == 2:
-                return four_sums[m][:]
-            return ten_sums[m][:]
+                return [four_sums[m][:]]
+            return [four_sums[3 * m][:], four_sums[3 * m + 1][:], pair_sums[2][:, m, :]]
 
         def front(i, first, count):
             grouped = stage.tile([P, CHUNK * D], BF16, tag="grouped", align_bytes=64)
@@ -136,9 +127,17 @@ def tile_contractexpand_pa_e_kernel(tc, inputs_c_e, Ws_words, Ws_scales, bs, out
             else:
                 for a in range(count):
                     flipped = psum_t.tile([P, PACK, P], F32, tag="flipped")
-                    source = summed(i, first + a)
+                    sources = summed(i, first + a)
                     for t in range(PACK):
-                        nc.tensor.transpose(flipped[:, t, :], source[:, t * P : (t + 1) * P], ident[:])
+                        for s, source in enumerate(sources):
+                            nc.tensor.matmul(
+                                out=flipped[:, t, :],
+                                lhsT=source[:, t * P : (t + 1) * P],
+                                rhs=ident[:],
+                                is_transpose=True,
+                                start=(s == 0),
+                                stop=(s == len(sources) - 1),
+                            )
                     nc.scalar.copy(
                         out=grouped[:, a * D : (a + 1) * D].rearrange("q (r t) -> q r t", t=PACK),
                         in_=flipped[:].rearrange("q t r -> q r t"),
@@ -208,8 +207,6 @@ def tile_contractexpand_pa_e_kernel(tc, inputs_c_e, Ws_words, Ws_scales, bs, out
         for c, i, first, count in units:
             if i == 2:
                 sum_chunk(c)
-            if i == 3:
-                sum_ten(first)
             quantised = front(i, first, count)
             if waiting is not None:
                 back(*waiting)

@@ -23,6 +23,7 @@ GROUP_LENGTHS = (1, 2, 4, 10)
 ROWS_PER_PARTITION = N_ROWS // P
 CHUNK = 4
 CHUNKS = ROWS_PER_PARTITION // CHUNK
+LATE = 2
 
 FLOPS = 2 * sum(N_ROWS // r for r in GROUP_LENGTHS) * D * DO
 
@@ -37,6 +38,7 @@ def tile_contractexpand_pa_e_kernel(tc, inputs_c_e, Ws_words, Ws_scales, bs, out
     with ExitStack() as ctx:
         keep = ctx.enter_context(tc.tile_pool(name="keep", bufs=1))
         stage = ctx.enter_context(tc.tile_pool(name="stage", bufs=4))
+        wide = ctx.enter_context(tc.tile_pool(name="wide", bufs=1))
         psum_t = ctx.enter_context(tc.psum_pool(name="psum_t", bufs=4))
         psum_mm = ctx.enter_context(tc.psum_pool(name="psum_mm", bufs=4))
 
@@ -155,7 +157,11 @@ def tile_contractexpand_pa_e_kernel(tc, inputs_c_e, Ws_words, Ws_scales, bs, out
             r = GROUP_LENGTHS[i]
             if first == 0:
                 spread_bias(i)
-            biased = keep.tile([P, count, DO], F32, name="biased%d_%d" % (i, first))
+            late = 1 < r < max(GROUP_LENGTHS) and first * r // CHUNK >= LATE
+            if late or r == max(GROUP_LENGTHS):
+                biased = stage.tile([P, count, DO], F32, tag="biased")
+            else:
+                biased = keep.tile([P, count, DO], F32, name="biased%d_%d" % (i, first))
             for a in range(count):
                 acc = psum_mm.tile([P, DO], F32, tag="acc")
                 nc.tensor.matmul_mx(
@@ -169,7 +175,7 @@ def tile_contractexpand_pa_e_kernel(tc, inputs_c_e, Ws_words, Ws_scales, bs, out
                 )
                 nc.vector.tensor_tensor(out=biased[:, a, :], in0=acc[:], in1=biases[i][:], op=ADD)
             if r == max(GROUP_LENGTHS):
-                repeated = keep.tile([P, r, DO], F32, name="repeated%d" % first)
+                repeated = wide.tile([P, r, DO], F32, tag="ten")
                 nc.vector.tensor_scalar(
                     out=repeated[:],
                     in0=biased[:].to_broadcast([P, r, DO]),
@@ -179,6 +185,20 @@ def tile_contractexpand_pa_e_kernel(tc, inputs_c_e, Ws_words, Ws_scales, bs, out
                     op1=MULT,
                 )
                 nc.sync.dma_start(out=out_rows[i][:, first * r : (first + 1) * r, :], in_=repeated[:])
+                return
+            if late:
+                rows = stage.tile([P, CHUNK, DO], F32, tag="rows")
+                for a in range(count):
+                    source = biased[:, a : a + 1, :].to_broadcast([P, r, DO])
+                    if count == 1:
+                        nc.vector.tensor_scalar(
+                            out=rows[:], in0=source, scalar1=0.0, scalar2=1.0 / r, op0=MAX, op1=MULT
+                        )
+                    else:
+                        nc.scalar.activation(
+                            out=rows[:, a * r : (a + 1) * r, :], in_=source, func=RELU, scale=1.0 / r
+                        )
+                nc.sync.dma_start(out=out_rows[i][:, first * r : first * r + CHUNK, :], in_=rows[:])
                 return
             nc.scalar.activation(out=biased[:], in_=biased[:], func=RELU, scale=1.0 / r)
             if r == 1:

@@ -23,7 +23,7 @@ GROUP_LENGTHS = (1, 2, 4, 10)
 ROWS_PER_PARTITION = N_ROWS // P
 CHUNK = 4
 CHUNKS = ROWS_PER_PARTITION // CHUNK
-LATE = 2
+LATE = 3
 
 FLOPS = 2 * sum(N_ROWS // r for r in GROUP_LENGTHS) * D * DO
 
@@ -38,7 +38,7 @@ def tile_contractexpand_pa_e_kernel(tc, inputs_c_e, Ws_words, Ws_scales, bs, out
     with ExitStack() as ctx:
         keep = ctx.enter_context(tc.tile_pool(name="keep", bufs=1))
         stage = ctx.enter_context(tc.tile_pool(name="stage", bufs=4))
-        wide = ctx.enter_context(tc.tile_pool(name="wide", bufs=1))
+        brief = ctx.enter_context(tc.tile_pool(name="brief", bufs=2))
         psum_t = ctx.enter_context(tc.psum_pool(name="psum_t", bufs=4))
         psum_mm = ctx.enter_context(tc.psum_pool(name="psum_mm", bufs=4))
 
@@ -159,7 +159,7 @@ def tile_contractexpand_pa_e_kernel(tc, inputs_c_e, Ws_words, Ws_scales, bs, out
                 spread_bias(i)
             late = 1 < r < max(GROUP_LENGTHS) and first * r // CHUNK >= LATE
             if late or r == max(GROUP_LENGTHS):
-                biased = stage.tile([P, count, DO], F32, tag="biased")
+                biased = brief.tile([P, count, DO], F32, tag="biased")
             else:
                 biased = keep.tile([P, count, DO], F32, name="biased%d_%d" % (i, first))
             for a in range(count):
@@ -175,7 +175,7 @@ def tile_contractexpand_pa_e_kernel(tc, inputs_c_e, Ws_words, Ws_scales, bs, out
                 )
                 nc.vector.tensor_tensor(out=biased[:, a, :], in0=acc[:], in1=biases[i][:], op=ADD)
             if r == max(GROUP_LENGTHS):
-                repeated = wide.tile([P, r, DO], F32, tag="ten")
+                repeated = keep.tile([P, r, DO], F32, name="repeated%d" % first)
                 nc.vector.tensor_scalar(
                     out=repeated[:],
                     in0=biased[:].to_broadcast([P, r, DO]),
@@ -187,7 +187,7 @@ def tile_contractexpand_pa_e_kernel(tc, inputs_c_e, Ws_words, Ws_scales, bs, out
                 nc.sync.dma_start(out=out_rows[i][:, first * r : (first + 1) * r, :], in_=repeated[:])
                 return
             if late:
-                rows = stage.tile([P, CHUNK, DO], F32, tag="rows")
+                rows = keep.tile([P, CHUNK, DO], F32, name="rows%d_%d" % (i, first))
                 for a in range(count):
                     source = biased[:, a : a + 1, :].to_broadcast([P, r, DO])
                     if count == 1:

@@ -23,7 +23,7 @@ GROUP_LENGTHS = (1, 2, 4, 10)
 ROWS_PER_PARTITION = N_ROWS // P
 CHUNK = 4
 CHUNKS = ROWS_PER_PARTITION // CHUNK
-LATE = 3
+LATE = 2
 
 FLOPS = 2 * sum(N_ROWS // r for r in GROUP_LENGTHS) * D * DO
 
@@ -39,6 +39,7 @@ def tile_contractexpand_pa_e_kernel(tc, inputs_c_e, Ws_words, Ws_scales, bs, out
         keep = ctx.enter_context(tc.tile_pool(name="keep", bufs=1))
         stage = ctx.enter_context(tc.tile_pool(name="stage", bufs=4))
         brief = ctx.enter_context(tc.tile_pool(name="brief", bufs=2))
+        last = ctx.enter_context(tc.tile_pool(name="last", bufs=4))
         psum_t = ctx.enter_context(tc.psum_pool(name="psum_t", bufs=4))
         psum_mm = ctx.enter_context(tc.psum_pool(name="psum_mm", bufs=4))
 
@@ -160,6 +161,8 @@ def tile_contractexpand_pa_e_kernel(tc, inputs_c_e, Ws_words, Ws_scales, bs, out
             late = 1 < r < max(GROUP_LENGTHS) and first * r // CHUNK >= LATE
             if late or r == max(GROUP_LENGTHS):
                 biased = brief.tile([P, count, DO], F32, tag="biased")
+            elif r == 1:
+                biased = last.tile([P, count, DO], F32, tag="x_rows")
             else:
                 biased = keep.tile([P, count, DO], F32, name="biased%d_%d" % (i, first))
             for a in range(count):

@@ -24,6 +24,8 @@ ROWS_PER_PARTITION = N_ROWS // P
 CHUNK = 4
 CHUNKS = ROWS_PER_PARTITION // CHUNK
 LATE = 2
+X_TILES = 2
+HEAD = 2
 
 FLOPS = 2 * sum(N_ROWS // r for r in GROUP_LENGTHS) * D * DO
 
@@ -39,14 +41,13 @@ def tile_contractexpand_pa_e_kernel(tc, inputs_c_e, Ws_words, Ws_scales, bs, out
         keep = ctx.enter_context(tc.tile_pool(name="keep", bufs=1))
         stage = ctx.enter_context(tc.tile_pool(name="stage", bufs=4))
         brief = ctx.enter_context(tc.tile_pool(name="brief", bufs=2))
-        last = ctx.enter_context(tc.tile_pool(name="last", bufs=4))
         psum_t = ctx.enter_context(tc.psum_pool(name="psum_t", bufs=4))
         psum_mm = ctx.enter_context(tc.psum_pool(name="psum_mm", bufs=4))
 
+        bias_row = keep.tile([P, scales_n * DO], BF16, name="bias_row")
+        nc.vector.memset(bias_row[:].bitcast(I32), 0)
         w_planes = keep.tile([P, DO], U8, name="w_planes", align_bytes=64)
         nc.vector.memset(w_planes[:].bitcast(I32), 0)
-        bias_row = keep.tile([P, scales_n * DO], BF16, name="bias_row")
-        nc.vector.memset(bias_row[:], 0.0)
         ones = keep.tile([P, P], BF16, name="ones")
         nc.vector.memset(ones[:], 1.0)
         ident = keep.tile([P, P], F32, name="ident")
@@ -55,8 +56,9 @@ def tile_contractexpand_pa_e_kernel(tc, inputs_c_e, Ws_words, Ws_scales, bs, out
         x_chunks = [keep.tile([P, CHUNK, D], BF16, name="x%d" % c) for c in range(CHUNKS)]
         w_words = [keep.tile([P, DO], U32, name="w%d" % g, align_bytes=64) for g in range(scales_n)]
 
-        def load_x(c):
-            nc.sync.dma_start(out=x_chunks[c][:], in_=x_rows[:, c * CHUNK : (c + 1) * CHUNK, :])
+        def load_x(c, first=0, count=CHUNK):
+            row = c * CHUNK + first
+            nc.sync.dma_start(out=x_chunks[c][:, first : first + count, :], in_=x_rows[:, row : row + count, :])
 
         def load_w(g):
             nc.sync.dma_start(
@@ -64,45 +66,61 @@ def tile_contractexpand_pa_e_kernel(tc, inputs_c_e, Ws_words, Ws_scales, bs, out
                 in_=Ws_words[g].rearrange("p n t -> p (n t)").bitcast(I32),
             )
 
-        load_x(0)
+        load_x(0, 0, 2)
+        nc.sync.dma_start(out=bias_row[0:1, :], in_=bs.rearrange("(o i) n -> o (i n)", o=1))
+        load_x(0, 2, 2)
+        load_w(1)
+        load_x(1)
         for quad in range(4):
             nc.sync.dma_start(
                 out=w_planes[32 * quad : 32 * quad + 16, :].bitcast(I32),
                 in_=Ws_scales[:, 4 * quad : 4 * quad + 4, :].bitcast(I32),
             )
-        nc.sync.dma_start(out=bias_row[0:1, :], in_=bs.rearrange("(o i) n -> o (i n)", o=1))
         load_w(2)
-        load_w(1)
-        load_x(1)
         load_x(2)
         load_w(3)
         load_x(3)
         load_x(4)
         load_w(0)
 
-        biases = [keep.tile([P, DO], F32, name="bias%d" % i) for i in range(scales_n)]
+        biases = {}
 
         def spread_bias(i):
             spread = psum_mm.tile([P, DO], F32, tag="acc")
             nc.tensor.matmul(
                 out=spread[:], lhsT=ones[:], rhs=bias_row[:, i * DO : (i + 1) * DO], start=True, stop=True
             )
+            biases[i] = keep.tile([P, DO], F32, name="bias%d" % i)
             nc.scalar.copy(out=biases[i][:], in_=spread[:])
 
         pair_sums = [keep.tile([P, CHUNK // 2, D], F32, name="pair%d" % c) for c in range(CHUNKS)]
         four_sums = [keep.tile([P, D], F32, name="four%d" % c) for c in range(CHUNKS)]
+        summed_pairs = set()
 
-        def sum_chunk(c):
+        def sum_pairs(c, first, count):
             halves = x_chunks[c][:].rearrange("p (m e) (q t) -> p e m t q", e=2, t=PACK)
             nc.vector.tensor_tensor(
-                out=pair_sums[c][:].rearrange("p m (t q) -> p m t q", t=PACK),
-                in0=halves[:, 0],
-                in1=halves[:, 1],
+                out=pair_sums[c][:, first : first + count, :].rearrange("p m (t q) -> p m t q", t=PACK),
+                in0=halves[:, 0, first : first + count],
+                in1=halves[:, 1, first : first + count],
                 op=ADD,
             )
-            nc.vector.tensor_tensor(
-                out=four_sums[c][:], in0=pair_sums[c][:, 0, :], in1=pair_sums[c][:, 1, :], op=ADD
-            )
+            summed_pairs.update(range(2 * c + first, 2 * c + first + count))
+
+        def sums(i, first, count):
+            r = GROUP_LENGTHS[i]
+            if r == 1:
+                return
+            for m in range(first * r // 2, (first + count) * r // 2):
+                if m not in summed_pairs:
+                    c = m // 2
+                    if c < LATE:
+                        sum_pairs(c, m % 2, 1)
+                    elif m % 2 == 0:
+                        sum_pairs(c, 0, 2)
+            if r == 4:
+                pair = pair_sums[first]
+                nc.vector.tensor_tensor(out=four_sums[first][:], in0=pair[:, 0, :], in1=pair[:, 1, :], op=ADD)
 
         def summed(i, m):
             if i == 1:
@@ -111,60 +129,71 @@ def tile_contractexpand_pa_e_kernel(tc, inputs_c_e, Ws_words, Ws_scales, bs, out
                 return [four_sums[m][:]]
             return [four_sums[3 * m][:], four_sums[3 * m + 1][:], pair_sums[2][:, m, :]]
 
-        def front(i, first, count):
-            grouped = stage.tile([P, CHUNK * D], BF16, tag="grouped", align_bytes=64)
+        grouped_of = {}
+
+        def turn(i, first, count):
+            grouped = stage.tile([P, 2 * D], BF16, tag="grouped", align_bytes=64)
+            grouped_of[(i, first)] = grouped
             if i == 0:
-                for b in range(count // 2):
-                    flipped = psum_t.tile([P, 4, P], F32, tag="flipped")
-                    for a in range(2):
-                        row = first + 2 * b + a
-                        words = x_chunks[row // CHUNK][:, row % CHUNK, :].bitcast(F32)
-                        for u in range(2):
-                            nc.tensor.transpose(flipped[:, 2 * a + u, :], words[:, u : D // 2 : 2], ident[:])
-                    nc.scalar.copy(
-                        out=grouped[:, 2 * b * D : 2 * (b + 1) * D]
-                        .bitcast(F32)
-                        .rearrange("q (a r u) -> q a r u", a=2, u=2),
-                        in_=flipped[:].rearrange("q (a u) r -> q a r u", u=2),
-                    )
-            else:
-                for a in range(count):
-                    flipped = psum_t.tile([P, PACK, P], F32, tag="flipped")
-                    sources = summed(i, first + a)
-                    for t in range(PACK):
-                        for s, source in enumerate(sources):
-                            nc.tensor.matmul(
-                                out=flipped[:, t, :],
-                                lhsT=source[:, t * P : (t + 1) * P],
-                                rhs=ident[:],
-                                is_transpose=True,
-                                start=(s == 0),
-                                stop=(s == len(sources) - 1),
-                            )
-                    nc.scalar.copy(
-                        out=grouped[:, a * D : (a + 1) * D].rearrange("q (r t) -> q r t", t=PACK),
-                        in_=flipped[:].rearrange("q t r -> q r t"),
-                    )
-            codes = stage.tile([P, CHUNK * P], U32, tag="codes", align_bytes=64)
-            planes = stage.tile([P, CHUNK * P], U8, tag="planes", align_bytes=64)
+                flipped = psum_t.tile([P, 4, P], F32, tag="flipped")
+                for a in range(2):
+                    row = first + a
+                    words = x_chunks[row // CHUNK][:, row % CHUNK, :].bitcast(F32)
+                    for u in range(2):
+                        nc.tensor.transpose(flipped[:, 2 * a + u, :], words[:, u : D // 2 : 2], ident[:])
+                nc.scalar.copy(
+                    out=grouped[:].bitcast(F32).rearrange("q (a r u) -> q a r u", a=2, u=2),
+                    in_=flipped[:].rearrange("q (a u) r -> q a r u", u=2),
+                )
+                return
+            for a in range(count):
+                flipped = psum_t.tile([P, PACK, P], F32, tag="flipped")
+                sources = summed(i, first + a)
+                for t in range(PACK):
+                    for s, source in enumerate(sources):
+                        nc.tensor.matmul(
+                            out=flipped[:, t, :],
+                            lhsT=source[:, t * P : (t + 1) * P],
+                            rhs=ident[:],
+                            is_transpose=True,
+                            start=(s == 0),
+                            stop=(s == len(sources) - 1),
+                        )
+                nc.scalar.copy(
+                    out=grouped[:, a * D : (a + 1) * D].rearrange("q (r t) -> q r t", t=PACK),
+                    in_=flipped[:].rearrange("q t r -> q r t"),
+                )
+
+        quantised_of = {}
+
+        def quantise(i, first, count):
+            codes = stage.tile([P, 2 * P], U32, tag="codes", align_bytes=64)
+            planes = stage.tile([P, 2 * P], U8, tag="planes", align_bytes=64)
             nc.vector.quantize_mx(
                 out=codes[:, : count * P].bitcast(FP8X4),
                 scales=planes[:, : count * P],
-                in_=grouped[:, : count * D],
+                in_=grouped_of[(i, first)][:, : count * D],
             )
-            return codes, planes
+            quantised_of[(i, first)] = (codes, planes)
 
-        def back(i, first, count, codes, planes):
+        x_results = {}
+
+        def finish(i, first, count):
             r = GROUP_LENGTHS[i]
-            if first == 0:
-                spread_bias(i)
+            codes, planes = quantised_of[(i, first)]
             late = 1 < r < max(GROUP_LENGTHS) and first * r // CHUNK >= LATE
-            if late or r == max(GROUP_LENGTHS):
-                biased = brief.tile([P, count, DO], F32, tag="biased")
+            long_run = r == max(GROUP_LENGTHS) and first > 0
+            if late or long_run:
+                biased = brief.tile([P, 2, DO], F32, tag="biased")
+                biased = biased[:, :count, :]
             elif r == 1:
-                biased = last.tile([P, count, DO], F32, tag="x_rows")
+                c = first // CHUNK
+                if c not in x_results:
+                    x_results[c] = keep.tile([P, CHUNK, DO], F32, name="x_rows%d" % c)
+                biased = x_results[c][:, first % CHUNK : first % CHUNK + count, :]
             else:
                 biased = keep.tile([P, count, DO], F32, name="biased%d_%d" % (i, first))
+                biased = biased[:]
             for a in range(count):
                 acc = psum_mm.tile([P, DO], F32, tag="acc")
                 nc.tensor.matmul_mx(
@@ -177,11 +206,11 @@ def tile_contractexpand_pa_e_kernel(tc, inputs_c_e, Ws_words, Ws_scales, bs, out
                     stop=True,
                 )
                 nc.vector.tensor_tensor(out=biased[:, a, :], in0=acc[:], in1=biases[i][:], op=ADD)
-            if r == max(GROUP_LENGTHS):
+            if long_run:
                 repeated = keep.tile([P, r, DO], F32, name="repeated%d" % first)
                 nc.vector.tensor_scalar(
                     out=repeated[:],
-                    in0=biased[:].to_broadcast([P, r, DO]),
+                    in0=biased.to_broadcast([P, r, DO]),
                     scalar1=0.0,
                     scalar2=1.0 / r,
                     op0=MAX,
@@ -203,9 +232,11 @@ def tile_contractexpand_pa_e_kernel(tc, inputs_c_e, Ws_words, Ws_scales, bs, out
                         )
                 nc.sync.dma_start(out=out_rows[i][:, first * r : first * r + CHUNK, :], in_=rows[:])
                 return
-            nc.scalar.activation(out=biased[:], in_=biased[:], func=RELU, scale=1.0 / r)
+            nc.scalar.activation(out=biased, in_=biased, func=RELU, scale=1.0 / r)
             if r == 1:
-                nc.sync.dma_start(out=out_rows[i][:, first : first + count, :], in_=biased[:])
+                if (first + count) % CHUNK == 0:
+                    c = first // CHUNK
+                    nc.sync.dma_start(out=out_rows[i][:, c * CHUNK : (c + 1) * CHUNK, :], in_=x_results[c][:])
             else:
                 for a in range(count):
                     m = first + a
@@ -214,24 +245,25 @@ def tile_contractexpand_pa_e_kernel(tc, inputs_c_e, Ws_words, Ws_scales, bs, out
                         in_=biased[:, a : a + 1, :].to_broadcast([P, r, DO]),
                     )
 
-        def units_of(c, i):
-            r = GROUP_LENGTHS[i]
-            ready = [m for m in range(ROWS_PER_PARTITION // r) if (m * r + r - 1) // CHUNK == c]
-            return [(c, i, ready[0], len(ready))] if ready else []
+        units = [(1, 0, 1), (2, 0, 1), (1, 1, 1), (2, 1, 1), (1, 2, 1), (3, 0, 1), (1, 3, 1)]
+        for c in range(2, CHUNKS):
+            units += [(2, c, 1), (1, 2 * c, 2)]
+        units.append((3, 1, 1))
+        units += [(0, first, X_TILES) for first in range(0, ROWS_PER_PARTITION, X_TILES)]
 
-        units = []
-        for c in range(CHUNKS):
-            for i in (2, 1, 3):
-                units.extend(units_of(c, i))
-        for c in range(CHUNKS):
-            units.extend(units_of(c, 0))
-
-        waiting = None
-        for c, i, first, count in units:
-            if i == 2:
-                sum_chunk(c)
-            quantised = front(i, first, count)
-            if waiting is not None:
-                back(*waiting)
-            waiting = (i, first, count) + quantised
-        back(*waiting)
+        with tc.manual_schedule():
+            for i in (1, 2):
+                spread_bias(i)
+            for stage_of in (sums, turn, quantise, finish):
+                for unit in units[:HEAD]:
+                    stage_of(*unit)
+        for i in (3, 0):
+            spread_bias(i)
+        for step in range(HEAD - 1, len(units)):
+            if step + 1 < len(units):
+                unit = units[step + 1]
+                sums(*unit)
+                turn(*unit)
+                quantise(*unit)
+            if step >= HEAD:
+                finish(*units[step])

@@ -23,7 +23,8 @@ GROUP_LENGTHS = (1, 2, 4, 10)
 ROWS_PER_PARTITION = N_ROWS // P
 CHUNK = 4
 CHUNKS = ROWS_PER_PARTITION // CHUNK
-LATE = 2
+SINGLE = 2
+DIRECT_ROWS = 8
 X_TILES = 2
 HEAD = 2
 
@@ -114,7 +115,7 @@ def tile_contractexpand_pa_e_kernel(tc, inputs_c_e, Ws_words, Ws_scales, bs, out
             for m in range(first * r // 2, (first + count) * r // 2):
                 if m not in summed_pairs:
                     c = m // 2
-                    if c < LATE:
+                    if c < SINGLE:
                         sum_pairs(c, m % 2, 1)
                     elif m % 2 == 0:
                         sum_pairs(c, 0, 2)
@@ -181,7 +182,7 @@ def tile_contractexpand_pa_e_kernel(tc, inputs_c_e, Ws_words, Ws_scales, bs, out
         def finish(i, first, count):
             r = GROUP_LENGTHS[i]
             codes, planes = quantised_of[(i, first)]
-            late = 1 < r < max(GROUP_LENGTHS) and first * r // CHUNK >= LATE
+            late = 1 < r < max(GROUP_LENGTHS) and (first + count) * r > DIRECT_ROWS
             long_run = r == max(GROUP_LENGTHS) and first > 0
             if late or long_run:
                 biased = brief.tile([P, 2, DO], F32, tag="biased")
@@ -219,10 +220,10 @@ def tile_contractexpand_pa_e_kernel(tc, inputs_c_e, Ws_words, Ws_scales, bs, out
                 nc.sync.dma_start(out=out_rows[i][:, first * r : (first + 1) * r, :], in_=repeated[:])
                 return
             if late:
-                rows = keep.tile([P, CHUNK, DO], F32, name="rows%d_%d" % (i, first))
+                rows = keep.tile([P, count * r, DO], F32, name="rows%d_%d" % (i, first))
                 for a in range(count):
                     source = biased[:, a : a + 1, :].to_broadcast([P, r, DO])
-                    if count == 1:
+                    if r == 4:
                         nc.vector.tensor_scalar(
                             out=rows[:], in0=source, scalar1=0.0, scalar2=1.0 / r, op0=MAX, op1=MULT
                         )
@@ -230,7 +231,17 @@ def tile_contractexpand_pa_e_kernel(tc, inputs_c_e, Ws_words, Ws_scales, bs, out
                         nc.scalar.activation(
                             out=rows[:, a * r : (a + 1) * r, :], in_=source, func=RELU, scale=1.0 / r
                         )
-                nc.sync.dma_start(out=out_rows[i][:, first * r : first * r + CHUNK, :], in_=rows[:])
+                nc.sync.dma_start(out=out_rows[i][:, first * r : (first + count) * r, :], in_=rows[:])
+                return
+            if r == max(GROUP_LENGTHS):
+                twice = keep.tile([P, 2, DO], F32, name="twice")
+                nc.scalar.activation(
+                    out=twice[:], in_=biased.to_broadcast([P, 2, DO]), func=RELU, scale=1.0 / r
+                )
+                nc.sync.dma_start(
+                    out=out_rows[i][:, :r, :].rearrange("p (b a) n -> p b (a n)", a=2),
+                    in_=twice[:].rearrange("p (o a) n -> p o (a n)", o=1).to_broadcast([P, r // 2, 2 * DO]),
+                )
                 return
             nc.scalar.activation(out=biased, in_=biased, func=RELU, scale=1.0 / r)
             if r == 1:

@@ -25,6 +25,7 @@ CHUNK = 4
 CHUNKS = ROWS_PER_PARTITION // CHUNK
 SINGLE = 2
 DIRECT_ROWS = 8
+X_STORE = 8
 X_TILES = 2
 HEAD = 2
 
@@ -188,10 +189,11 @@ def tile_contractexpand_pa_e_kernel(tc, inputs_c_e, Ws_words, Ws_scales, bs, out
                 biased = brief.tile([P, 2, DO], F32, tag="biased")
                 biased = biased[:, :count, :]
             elif r == 1:
-                c = first // CHUNK
+                c = first // X_STORE
                 if c not in x_results:
-                    x_results[c] = keep.tile([P, CHUNK, DO], F32, name="x_rows%d" % c)
-                biased = x_results[c][:, first % CHUNK : first % CHUNK + count, :]
+                    rows_n = min(X_STORE, ROWS_PER_PARTITION - c * X_STORE)
+                    x_results[c] = keep.tile([P, rows_n, DO], F32, name="x_rows%d" % c)
+                biased = x_results[c][:, first % X_STORE : first % X_STORE + count, :]
             else:
                 biased = keep.tile([P, count, DO], F32, name="biased%d_%d" % (i, first))
                 biased = biased[:]
@@ -245,9 +247,10 @@ def tile_contractexpand_pa_e_kernel(tc, inputs_c_e, Ws_words, Ws_scales, bs, out
                 return
             nc.scalar.activation(out=biased, in_=biased, func=RELU, scale=1.0 / r)
             if r == 1:
-                if (first + count) % CHUNK == 0:
-                    c = first // CHUNK
-                    nc.sync.dma_start(out=out_rows[i][:, c * CHUNK : (c + 1) * CHUNK, :], in_=x_results[c][:])
+                last = first + count
+                if last % X_STORE == 0 or last == ROWS_PER_PARTITION:
+                    c = first // X_STORE
+                    nc.sync.dma_start(out=out_rows[i][:, c * X_STORE : last, :], in_=x_results[c][:])
             else:
                 for a in range(count):
                     m = first + a

from contextlib import ExitStack

from concourse import mybir
from concourse.masks import make_identity

F32 = mybir.dt.float32
BF16 = mybir.dt.bfloat16
I32 = mybir.dt.int32
U32 = mybir.dt.uint32
U8 = mybir.dt.uint8
FP8X4 = mybir.dt.float8_e4m3fn_x4
ADD = mybir.AluOpType.add
MAX = mybir.AluOpType.max
MULT = mybir.AluOpType.mult
RELU = mybir.ActivationFunctionType.Relu

P = 128
PACK = 4
N_ROWS = 2560
D = 512
DO = 512
GROUP_LENGTHS = (1, 2, 4, 10)
ROWS_PER_PARTITION = N_ROWS // P
CHUNK = 4
CHUNKS = ROWS_PER_PARTITION // CHUNK
SINGLE = 2
DIRECT_ROWS = 8
X_STORE = 8
X_TILES = 2
HEAD = 2

FLOPS = 2 * sum(N_ROWS // r for r in GROUP_LENGTHS) * D * DO


def tile_contractexpand_pa_e_kernel(tc, inputs_c_e, Ws_words, Ws_scales, bs, out):
    nc = tc.nc
    scales_n = len(GROUP_LENGTHS)

    x_rows = inputs_c_e.rearrange("(p j) d -> p j d", j=ROWS_PER_PARTITION)
    out_rows = out.rearrange("(i p j) n -> i p j n", i=scales_n, j=ROWS_PER_PARTITION)

    with ExitStack() as ctx:
        keep = ctx.enter_context(tc.tile_pool(name="keep", bufs=1))
        stage = ctx.enter_context(tc.tile_pool(name="stage", bufs=4))
        brief = ctx.enter_context(tc.tile_pool(name="brief", bufs=2))
        psum_t = ctx.enter_context(tc.psum_pool(name="psum_t", bufs=4))
        psum_mm = ctx.enter_context(tc.psum_pool(name="psum_mm", bufs=4))

        bias_row = keep.tile([P, scales_n * DO], BF16, name="bias_row")
        nc.vector.memset(bias_row[:].bitcast(I32), 0)
        w_planes = keep.tile([P, DO], U8, name="w_planes", align_bytes=64)
        nc.vector.memset(w_planes[:].bitcast(I32), 0)
        ones = keep.tile([P, P], BF16, name="ones")
        nc.vector.memset(ones[:], 1.0)
        ident = keep.tile([P, P], F32, name="ident")
        make_identity(nc, ident[:])

        x_chunks = [keep.tile([P, CHUNK, D], BF16, name="x%d" % c) for c in range(CHUNKS)]
        w_words = [keep.tile([P, DO], U32, name="w%d" % g, align_bytes=64) for g in range(scales_n)]

        def load_x(c, first=0, count=CHUNK):
            row = c * CHUNK + first
            nc.sync.dma_start(out=x_chunks[c][:, first : first + count, :], in_=x_rows[:, row : row + count, :])

        def load_w(g):
            nc.sync.dma_start(
                out=w_words[g][:].bitcast(I32),
                in_=Ws_words[g].rearrange("p n t -> p (n t)").bitcast(I32),
            )

        load_x(0, 0, 2)
        nc.sync.dma_start(out=bias_row[0:1, :], in_=bs.rearrange("(o i) n -> o (i n)", o=1))
        load_x(0, 2, 2)
        load_w(1)
        load_x(1)
        for quad in range(4):
            nc.sync.dma_start(
                out=w_planes[32 * quad : 32 * quad + 16, :].bitcast(I32),
                in_=Ws_scales[:, 4 * quad : 4 * quad + 4, :].bitcast(I32),
            )
        load_w(2)
        load_x(2)
        load_w(3)
        load_x(3)
        load_x(4)
        load_w(0)

        biases = {}

        def spread_bias(i):
            spread = psum_mm.tile([P, DO], F32, tag="acc")
            nc.tensor.matmul(
                out=spread[:], lhsT=ones[:], rhs=bias_row[:, i * DO : (i + 1) * DO], start=True, stop=True
            )
            biases[i] = keep.tile([P, DO], F32, name="bias%d" % i)
            nc.scalar.copy(out=biases[i][:], in_=spread[:])

        pair_sums = [keep.tile([P, CHUNK // 2, D], F32, name="pair%d" % c) for c in range(CHUNKS)]
        four_sums = [keep.tile([P, D], F32, name="four%d" % c) for c in range(CHUNKS)]
        summed_pairs = set()

        def sum_pairs(c, first, count):
            halves = x_chunks[c][:].rearrange("p (m e) (q t) -> p e m t q", e=2, t=PACK)
            nc.vector.tensor_tensor(
                out=pair_sums[c][:, first : first + count, :].rearrange("p m (t q) -> p m t q", t=PACK),
                in0=halves[:, 0, first : first + count],
                in1=halves[:, 1, first : first + count],
                op=ADD,
            )
            summed_pairs.update(range(2 * c + first, 2 * c + first + count))

        def sums(i, first, count):
            r = GROUP_LENGTHS[i]
            if r == 1:
                return
            for m in range(first * r // 2, (first + count) * r // 2):
                if m not in summed_pairs:
                    c = m // 2
                    if c < SINGLE:
                        sum_pairs(c, m % 2, 1)
                    elif m % 2 == 0:
                        sum_pairs(c, 0, 2)
            if r == 4:
                pair = pair_sums[first]
                nc.vector.tensor_tensor(out=four_sums[first][:], in0=pair[:, 0, :], in1=pair[:, 1, :], op=ADD)

        def summed(i, m):
            if i == 1:
                return [pair_sums[m // 2][:, m % 2, :]]
            if i == 2:
                return [four_sums[m][:]]
            return [four_sums[3 * m][:], four_sums[3 * m + 1][:], pair_sums[2][:, m, :]]

        grouped_of = {}

        def turn(i, first, count):
            grouped = stage.tile([P, 2 * D], BF16, tag="grouped", align_bytes=64)
            grouped_of[(i, first)] = grouped
            if i == 0:
                flipped = psum_t.tile([P, 4, P], F32, tag="flipped")
                for a in range(2):
                    row = first + a
                    words = x_chunks[row // CHUNK][:, row % CHUNK, :].bitcast(F32)
                    for u in range(2):
                        nc.tensor.transpose(flipped[:, 2 * a + u, :], words[:, u : D // 2 : 2], ident[:])
                nc.scalar.copy(
                    out=grouped[:].bitcast(F32).rearrange("q (a r u) -> q a r u", a=2, u=2),
                    in_=flipped[:].rearrange("q (a u) r -> q a r u", u=2),
                )
                return
            for a in range(count):
                flipped = psum_t.tile([P, PACK, P], F32, tag="flipped")
                sources = summed(i, first + a)
                for t in range(PACK):
                    for s, source in enumerate(sources):
                        nc.tensor.matmul(
                            out=flipped[:, t, :],
                            lhsT=source[:, t * P : (t + 1) * P],
                            rhs=ident[:],
                            is_transpose=True,
                            start=(s == 0),
                            stop=(s == len(sources) - 1),
                        )
                nc.scalar.copy(
                    out=grouped[:, a * D : (a + 1) * D].rearrange("q (r t) -> q r t", t=PACK),
                    in_=flipped[:].rearrange("q t r -> q r t"),
                )

        quantised_of = {}

        def quantise(i, first, count):
            codes = stage.tile([P, 2 * P], U32, tag="codes", align_bytes=64)
            planes = stage.tile([P, 2 * P], U8, tag="planes", align_bytes=64)
            nc.vector.quantize_mx(
                out=codes[:, : count * P].bitcast(FP8X4),
                scales=planes[:, : count * P],
                in_=grouped_of[(i, first)][:, : count * D],
            )
            quantised_of[(i, first)] = (codes, planes)

        x_results = {}

        def finish(i, first, count):
            r = GROUP_LENGTHS[i]
            codes, planes = quantised_of[(i, first)]
            late = 1 < r < max(GROUP_LENGTHS) and (first + count) * r > DIRECT_ROWS
            long_run = r == max(GROUP_LENGTHS) and first > 0
            if late or long_run:
                biased = brief.tile([P, 2, DO], F32, tag="biased")
                biased = biased[:, :count, :]
            elif r == 1:
                c = first // X_STORE
                if c not in x_results:
                    rows_n = min(X_STORE, ROWS_PER_PARTITION - c * X_STORE)
                    x_results[c] = keep.tile([P, rows_n, DO], F32, name="x_rows%d" % c)
                biased = x_results[c][:, first % X_STORE : first % X_STORE + count, :]
            else:
                biased = keep.tile([P, count, DO], F32, name="biased%d_%d" % (i, first))
                biased = biased[:]
            for a in range(count):
                acc = psum_mm.tile([P, DO], F32, tag="acc")
                nc.tensor.matmul_mx(
                    out=acc[:],
                    lhsT=codes[:, a * P : (a + 1) * P].bitcast(FP8X4),
                    lhsT_scale=planes[:, a * P : (a + 1) * P],
                    rhs=w_words[i][:].bitcast(FP8X4),
                    rhs_scale=w_planes[4 * i : P, :],
                    start=True,
                    stop=True,
                )
                nc.vector.tensor_tensor(out=biased[:, a, :], in0=acc[:], in1=biases[i][:], op=ADD)
            if long_run:
                repeated = keep.tile([P, r, DO], F32, name="repeated%d" % first)
                nc.vector.tensor_scalar(
                    out=repeated[:],
                    in0=biased.to_broadcast([P, r, DO]),
                    scalar1=0.0,
                    scalar2=1.0 / r,
                    op0=MAX,
                    op1=MULT,
                )
                nc.sync.dma_start(out=out_rows[i][:, first * r : (first + 1) * r, :], in_=repeated[:])
                return
            if late:
                rows = keep.tile([P, count * r, DO], F32, name="rows%d_%d" % (i, first))
                for a in range(count):
                    source = biased[:, a : a + 1, :].to_broadcast([P, r, DO])
                    if r == 4:
                        nc.vector.tensor_scalar(
                            out=rows[:], in0=source, scalar1=0.0, scalar2=1.0 / r, op0=MAX, op1=MULT
                        )
                    else:
                        nc.scalar.activation(
                            out=rows[:, a * r : (a + 1) * r, :], in_=source, func=RELU, scale=1.0 / r
                        )
                nc.sync.dma_start(out=out_rows[i][:, first * r : (first + count) * r, :], in_=rows[:])
                return
            if r == max(GROUP_LENGTHS):
                twice = keep.tile([P, 2, DO], F32, name="twice")
                nc.scalar.activation(
                    out=twice[:], in_=biased.to_broadcast([P, 2, DO]), func=RELU, scale=1.0 / r
                )
                nc.sync.dma_start(
                    out=out_rows[i][:, :r, :].rearrange("p (b a) n -> p b (a n)", a=2),
                    in_=twice[:].rearrange("p (o a) n -> p o (a n)", o=1).to_broadcast([P, r // 2, 2 * DO]),
                )
                return
            nc.scalar.activation(out=biased, in_=biased, func=RELU, scale=1.0 / r)
            if r == 1:
                last = first + count
                if last % X_STORE == 0 or last == ROWS_PER_PARTITION:
                    c = first // X_STORE
                    nc.sync.dma_start(out=out_rows[i][:, c * X_STORE : last, :], in_=x_results[c][:])
            else:
                for a in range(count):
                    m = first + a
                    nc.sync.dma_start(
                        out=out_rows[i][:, m * r : (m + 1) * r, :],
                        in_=biased[:, a : a + 1, :].to_broadcast([P, r, DO]),
                    )

        units = [(1, 0, 1), (2, 0, 1), (1, 1, 1), (2, 1, 1), (1, 2, 1), (3, 0, 1), (1, 3, 1)]
        for c in range(2, CHUNKS):
            units += [(2, c, 1), (1, 2 * c, 2)]
        units.append((3, 1, 1))
        units += [(0, first, X_TILES) for first in range(0, ROWS_PER_PARTITION, X_TILES)]

        with tc.manual_schedule():
            for i in (1, 2):
                spread_bias(i)
            for stage_of in (sums, turn, quantise, finish):
                for unit in units[:HEAD]:
                    stage_of(*unit)
        for i in (3, 0):
            spread_bias(i)
        for step in range(HEAD - 1, len(units)):
            if step + 1 < len(units):
                unit = units[step + 1]
                sums(*unit)
                turn(*unit)
                quantise(*unit)
            if step >= HEAD:
                finish(*units[step])
